import numpy as np
import ml_dtypes


def mxq(x, axis, fmt="e4m3"):
    dtype, down = {"e4m3": (ml_dtypes.float8_e4m3fn, 7), "e5m2": (ml_dtypes.float8_e5m2, 14)}[fmt]
    v = np.moveaxis(np.asarray(x, np.float32).astype(ml_dtypes.bfloat16).astype(np.float64), axis, -1)
    blocks = v.reshape(v.shape[:-1] + (-1, 32))
    amax = np.abs(blocks).max(-1, keepdims=True)
    byte = np.maximum(np.where(amax > 0, np.frexp(amax)[1] - 1 + 127, 0) - down, 1)
    scale = np.exp2(byte - 127.0)
    codes = (blocks / scale).astype(np.float32).astype(dtype).astype(np.float64)
    return np.moveaxis((codes * scale).reshape(v.shape), -1, axis)


WIDE = False


def mx_kscale(k):
    if not WIDE:
        return np.ones(k)
    levels = np.array([10, -10, 5, -5, 0])
    if k % 512:
        return np.exp2(np.random.permutation(np.resize(levels, k // 32))).repeat(32)
    a = np.empty((k // 512, 16))
    for p in range(k // 512):
        a[p, :8] = np.random.permutation(np.resize(levels, 8))
        for g in range(8):
            far = levels[np.abs(levels - a[p, g]) >= 10]
            a[p, g + 8] = far[np.random.randint(len(far))]
    return np.exp2(a.ravel()).repeat(32)


BF16 = ml_dtypes.bfloat16


def bf(x):
    return np.asarray(x, np.float32).astype(BF16)


def f64(x):
    return np.asarray(x).astype(np.float64)


B, U, I, H = 256, 16, 512, 128


def sigmoid(v):
    return 1.0 / (1.0 + np.exp(-v))


def setup_inputs():
    s = mx_kscale(I)
    return {"inputs": bf(np.random.standard_normal((B, U, I)) * s),
            "hidden": bf(np.random.standard_normal((B, U, H))),
            "w_ih": bf(np.random.standard_normal((U, 3 * H, I)) / np.sqrt(I) / s),
            "w_hh": bf(np.random.standard_normal((U, 3 * H, H)) / np.sqrt(H)),
            "b_ih": bf(np.random.standard_normal((U, 3 * H)) * 0.3),
            "b_hh": bf(np.random.standard_normal((U, 3 * H)) * 0.3)}


def reference(inputs, hidden, w_ih, w_hh, b_ih, b_hh):
    h = f64(hidden)
    gx = (mxq(f64(inputs), 2, "e4m3").transpose(1, 0, 2) @ mxq(f64(w_ih), 2, "e4m3").transpose(0, 2, 1)).transpose(1, 0, 2) + f64(b_ih)
    gh = (h.transpose(1, 0, 2) @ f64(w_hh).transpose(0, 2, 1)).transpose(1, 0, 2) + f64(b_hh)
    xr, xz, xn = gx[..., :H], gx[..., H:2 * H], gx[..., 2 * H:]
    hr, hz, hn = gh[..., :H], gh[..., H:2 * H], gh[..., 2 * H:]
    r = sigmoid(xr + hr)
    z = sigmoid(xz + hz)
    n = np.tanh(xn + r * hn)
    return (1.0 - z) * n + z * h

@@ -1,0 +1,295 @@
+from contextlib import ExitStack
+
+import concourse.masks as masks
+import concourse.mybir as mybir
+
+F32 = mybir.dt.float32
+BF16 = mybir.dt.bfloat16
+U32 = mybir.dt.uint32
+U8 = mybir.dt.uint8
+FP8X4 = mybir.dt.float8_e4m3fn_x4
+ACT = mybir.ActivationFunctionType
+ALU = mybir.AluOpType
+
+P = 128
+B, U, I, H = 256, 16, 512, 128
+J = B // P
+GATES = 3
+PACK = 4
+WORDS = PACK // 2
+QUAD = 4
+FLOPS = 2 * B * U * GATES * H * (I + H)
+
+
+def tile_grouptorchgru_kernel(tc, inputs, hidden, w_ih, w_hh, b_ih, b_hh, out):
+    nc = tc.nc
+    x_view = inputs.rearrange("(j p) u k -> p j (u k)", p=P)
+    h_view = hidden.rearrange("(j p) u h -> p j (u h)", p=P)
+    out_view = out.rearrange("(j p) u h -> p j (u h)", p=P)
+    w_view = w_ih.flatten_outer_dims().rearrange("(g p) k -> p g k", p=P)
+    whh_view = w_hh.flatten_outer_dims().rearrange("(g p) k -> p g k", p=P)
+
+    with ExitStack() as ctx:
+        keep = ctx.enter_context(tc.tile_pool(name="keep", bufs=1))
+        stage = ctx.enter_context(tc.tile_pool(name="stage", bufs=2))
+        quant = ctx.enter_context(tc.tile_pool(name="quant", bufs=3))
+        work = ctx.enter_context(tc.tile_pool(name="work", bufs=3))
+        psum = ctx.enter_context(tc.psum_pool(name="psum", bufs=1))
+        ctx.enter_context(tc.manual_schedule())
+
+        bias_rows = keep.tile([P, P], BF16, name="bias_rows")
+        nc.scalar.dma_start(out=bias_rows[0:U * GATES, :], in_=b_ih.rearrange("u (g h) -> (u g) h", h=H))
+        nc.scalar.dma_start(out=bias_rows[U * GATES:2 * U * GATES, :],
+                            in_=b_hh.rearrange("u (g h) -> (u g) h", h=H))
+        nc.vector.memset(bias_rows[2 * U * GATES:P, :], 0.0)
+        warm = keep.tile([P, 2], F32, name="warm")
+        nc.vector.memset(warm[:], 0.0)
+        nc.scalar.activation(out=warm[:, 1:2], in_=warm[:, 0:1], func=ACT.Sigmoid)
+        ident_b = keep.tile([P, P], BF16, name="ident_b")
+        masks.make_identity(nc, ident_b[:])
+        ident_f = keep.tile([P, P], F32, name="ident_f")
+        masks.make_identity(nc, ident_f[:])
+
+        x_nat, w_nat, whh_nat, h_nat = [], [], [], []
+        for u in range(U):
+            x_nat.append(keep.tile([P, J, I], BF16, name="x_nat%d" % u))
+            nc.sync.dma_start(out=x_nat[u][:], in_=x_view[:, :, u * I:(u + 1) * I])
+            w_nat.append(keep.tile([P, GATES, I], BF16, name="w_nat%d" % u))
+            nc.sync.dma_start(out=w_nat[u][:], in_=w_view[:, u * GATES:(u + 1) * GATES, :])
+            if u % QUAD == 0:
+                h_nat.append(keep.tile([P, J, QUAD * H], BF16, name="h_nat%d" % (u // QUAD)))
+                nc.sync.dma_start(out=h_nat[u // QUAD][:], in_=h_view[:, :, u * H:(u + QUAD) * H])
+            whh_nat.append(keep.tile([P, GATES, H], BF16, name="whh_nat%d" % u))
+            nc.sync.dma_start(out=whh_nat[u][:], in_=whh_view[:, u * GATES:(u + 1) * GATES, :])
+
+        def hidden_rows(u):
+            return h_nat[u // QUAD][:, :, (u % QUAD) * H:(u % QUAD + 1) * H]
+
+        bias_ps = psum.tile([P, J + GATES, P], BF16, tag="hidden_t", name="bias_ps")
+        nc.tensor.transpose(bias_ps[:, 0, :], bias_rows[:], ident_b[:])
+        bias_cols = keep.tile([P, P], F32, name="bias_cols")
+        nc.vector.tensor_copy(out=bias_cols[:], in_=bias_ps[:, 0, :])
+        bias_sum = keep.tile([P, U * GATES], F32, name="bias_sum")
+        nc.vector.tensor_tensor(out=bias_sum[:], in0=bias_cols[:, 0:U * GATES],
+                                in1=bias_cols[:, U * GATES:2 * U * GATES], op=ALU.add)
+        bias_neg = keep.tile([P, U * GATES], F32, name="bias_neg")
+        nc.vector.tensor_scalar_mul(out=bias_neg[:], in0=bias_sum[:], scalar1=-1.0)
+
+        def column(table, index):
+            return table[:, index:index + 1]
+
+        made = {}
+
+        def absent(u):
+            return u < 0 or u >= U
+
+        def transpose_words(bank, rows):
+            for a in range(len(rows)):
+                for w in range(WORDS):
+                    nc.tensor.transpose(bank[:, a, w, :], rows[a].bitcast(F32)[:, w:WORDS * P:WORDS], ident_f[:])
+
+        def interleave(copy, grouped, bank):
+            copy(out=grouped.bitcast(F32).rearrange("p (a c w) -> p a c w", c=P, w=WORDS),
+                 in_=bank[:].rearrange("p a w c -> p a c w"))
+
+        def transpose_x(u):
+            if absent(u):
+                return
+            made["x_t", u] = psum.tile([P, J, WORDS, P], F32, tag="x_t", name="x_t")
+            transpose_words(made["x_t", u], [x_nat[u][:, j, :] for j in range(J)])
+
+        def transpose_w_rz(u):
+            if absent(u):
+                return
+            made["w_rz_t", u] = psum.tile([P, 2, WORDS, P], F32, tag="w_rz_t", name="w_rz_t")
+            transpose_words(made["w_rz_t", u], [w_nat[u][:, g, :] for g in range(2)])
+
+        def transpose_w_n(u):
+            if absent(u):
+                return
+            made["w_n_t", u] = psum.tile([P, 1, WORDS, P], F32, tag="w_n_t", name="w_n_t")
+            transpose_words(made["w_n_t", u], [w_nat[u][:, 2, :]])
+
+        def transpose_hidden(u):
+            if absent(u):
+                return
+            bank = psum.tile([P, J + GATES, P], BF16, tag="hidden_t", name="hidden_t")
+            for j in range(J):
+                nc.tensor.transpose(bank[:, j, :], hidden_rows(u)[:, j, :], ident_b[:])
+            for g in range(GATES):
+                nc.tensor.transpose(bank[:, J + g, :], whh_nat[u][:, g, :], ident_b[:])
+            made["hidden_t", u] = bank
+
+        def copy_x(u):
+            if absent(u):
+                return
+            made["x_w_rz", u] = stage.tile([P, (B + 2 * H) * PACK], BF16, name="x_w_rz", align_bytes=64)
+            interleave(nc.scalar.copy, made["x_w_rz", u][:, 0:B * PACK], made["x_t", u])
+
+        def copy_w_rz(u):
+            if absent(u):
+                return
+            interleave(nc.scalar.copy, made["x_w_rz", u][:, B * PACK:(B + 2 * H) * PACK], made["w_rz_t", u])
+
+        def copy_w_n(u):
+            if absent(u):
+                return
+            made["w_n", u] = stage.tile([P, H * PACK], BF16, name="w_n", align_bytes=64)
+            interleave(nc.vector.tensor_copy, made["w_n", u][:], made["w_n_t", u])
+
+        def copy_hidden(u):
+            if absent(u):
+                return
+            made["hidden", u] = keep.tile([P, J + GATES, P], BF16, name="hidden%d" % u)
+            copy = nc.scalar.copy if u % 2 == 0 else nc.vector.tensor_copy
+            copy(out=made["hidden", u][:], in_=made["hidden_t", u][:])
+
+        def hidden_t(u):
+            return made["hidden", u][:, 0:J, :].rearrange("p j b -> p (j b)")
+
+        def quantise(u, name):
+            if absent(u):
+                return
+            columns = made[name, u].shape[1] // PACK
+            codes = quant.tile([P, columns], U32, name=name + "_codes", align_bytes=64)
+            scales = quant.tile([P, columns], U8, name=name + "_scales", align_bytes=64)
+            nc.vector.quantize_mx(out=codes[:].bitcast(FP8X4), scales=scales[:], in_=made[name, u][:])
+            made[name + "_q", u] = (codes, scales)
+
+        def matmul_x(u, acc, weights, first):
+            x_codes, x_scales = made["x_w_rz_q", u]
+            w_codes, w_scales = weights
+            nc.tensor.matmul_mx(out=acc,
+                                lhsT=w_codes[:, first:first + H].bitcast(FP8X4),
+                                lhsT_scale=w_scales[:, first:first + H],
+                                rhs=x_codes[:, 0:B].bitcast(FP8X4), rhs_scale=x_scales[:, 0:B],
+                                start=True, stop=True)
+
+        def matmul_h(u, acc, g):
+            nc.tensor.matmul(out=acc, lhsT=made["hidden", u][:, J + g, :], rhs=hidden_t(u), start=True, stop=True)
+
+        def matmul_h_rz(u):
+            if absent(u):
+                return
+            made["h_rz", u] = psum.tile([P, 2 * B], F32, tag="h_rz", name="h_rz")
+            for g in range(2):
+                matmul_h(u, made["h_rz", u][:, g * B:(g + 1) * B], g)
+
+        def matmul_x_rz(u):
+            if absent(u):
+                return
+            made["x_rz", u] = psum.tile([P, 2 * B], F32, tag="x_rz", name="x_rz")
+            for g in range(2):
+                matmul_x(u, made["x_rz", u][:, g * B:(g + 1) * B], made["x_w_rz_q", u], B + g * H)
+
+        def matmul_n(u):
+            if absent(u):
+                return
+            made["hx_n", u] = psum.tile([P, 2 * B], F32, tag="hx_n", name="hx_n")
+            matmul_h(u, made["hx_n", u][:, 0:B], 2)
+            matmul_x(u, made["hx_n", u][:, B:2 * B], made["w_n_q", u], 0)
+
+        def copy_h_rz(u):
+            if absent(u):
+                return
+            made["h_rz_sb", u] = work.tile([P, 2 * B], F32, name="h_rz_sb")
+            nc.scalar.copy(out=made["h_rz_sb", u][:], in_=made["h_rz", u][:])
+
+        def add_rz(u):
+            if absent(u):
+                return
+            made["rz", u] = work.tile([P, 2 * B], F32, name="rz")
+            nc.vector.tensor_tensor(out=made["rz", u][:], in0=made["x_rz", u][:], in1=made["h_rz_sb", u][:],
+                                    op=ALU.add)
+
+        def reset_gate(u):
+            if absent(u):
+                return
+            made["r", u] = work.tile([P, B], F32, name="r")
+            nc.scalar.activation(out=made["r", u][:], in_=made["rz", u][:, 0:B], func=ACT.Sigmoid,
+                                 bias=column(bias_sum, u * GATES), scale=1.0)
+
+        def update_gate(u):
+            if absent(u):
+                return
+            made["one_minus_z", u] = work.tile([P, B], F32, name="one_minus_z")
+            nc.scalar.activation(out=made["one_minus_z", u][:], in_=made["rz", u][:, B:2 * B], func=ACT.Sigmoid,
+                                 bias=column(bias_neg, u * GATES + 1), scale=-1.0)
+
+        def reset_times_hn(u):
+            if absent(u):
+                return
+            made["r_hn", u] = work.tile([P, B], F32, name="r_hn")
+            nc.vector.scalar_tensor_tensor(out=made["r_hn", u][:], in0=made["hx_n", u][:, 0:B],
+                                           scalar=column(bias_cols, (U + u) * GATES + 2), in1=made["r", u][:],
+                                           op0=ALU.add, op1=ALU.mult)
+
+        def add_xn(u):
+            if absent(u):
+                return
+            made["n_sum", u] = work.tile([P, B], F32, name="n_sum")
+            nc.vector.tensor_tensor(out=made["n_sum", u][:], in0=made["hx_n", u][:, B:2 * B],
+                                    in1=made["r_hn", u][:], op=ALU.add)
+
+        def new_gate(u):
+            if absent(u):
+                return
+            made["n", u] = work.tile([P, B], F32, name="n")
+            nc.scalar.activation(out=made["n", u][:], in_=made["n_sum", u][:], func=ACT.Tanh,
+                                 bias=column(bias_cols, u * GATES + 2), scale=1.0)
+
+        def blend(u):
+            if absent(u):
+                return
+            engine = nc.gpsimd if u < U - 2 else nc.vector
+            made["n_minus_h", u] = work.tile([P, B], F32, name="n_minus_h")
+            engine.tensor_tensor(out=made["n_minus_h", u][:], in0=made["n", u][:], in1=hidden_t(u), op=ALU.subtract)
+            made["step", u] = work.tile([P, B], F32, name="step")
+            engine.tensor_tensor(out=made["step", u][:], in0=made["one_minus_z", u][:], in1=made["n_minus_h", u][:],
+                                 op=ALU.mult)
+
+        def transpose_back(u):
+            if absent(u):
+                return
+            made["step_t", u] = psum.tile([P, J, H], F32, tag="step_t", name="step_t")
+            for j in range(J):
+                nc.tensor.transpose(made["step_t", u][:, j, :], made["step", u][:, j * P:(j + 1) * P], ident_f[:])
+
+        def add_hidden_and_store(u):
+            if absent(u):
+                return
+            if u % 2 == 0:
+                made["out", u // 2] = keep.tile([P, J, 2 * H], F32, name="out%d" % (u // 2))
+            pair = made["out", u // 2]
+            nc.vector.tensor_tensor(out=pair[:, :, (u % 2) * H:(u % 2 + 1) * H], in0=made["step_t", u][:],
+                                    in1=hidden_rows(u), op=ALU.add)
+            if u % 2 == 1:
+                nc.sync.dma_start(out=out_view[:, :, (u - 1) * H:(u + 1) * H], in_=pair[:])
+
+        for i in range(-2, U + 3):
+            copy_x(i + 1)
+            copy_w_rz(i + 1)
+            copy_h_rz(i)
+            reset_gate(i - 1)
+            new_gate(i - 2)
+            copy_w_n(i + 1)
+            copy_hidden(i + 1)
+            update_gate(i - 2)
+
+            matmul_n(i - 1)
+            transpose_x(i + 2)
+            transpose_w_rz(i + 2)
+            transpose_back(i - 3)
+
+            quantise(i + 1, "x_w_rz")
+            quantise(i + 1, "w_n")
+            reset_times_hn(i - 1)
+            add_rz(i)
+            add_xn(i - 1)
+            blend(i - 2)
+            add_hidden_and_store(i - 3)
+
+            matmul_h_rz(i + 1)
+            transpose_w_n(i + 2)
+            transpose_hidden(i + 2)
+            matmul_x_rz(i + 1)

@@ -33,7 +33,7 @@ def tile_grouptorchgru_kernel(tc, inputs, hidden, w_ih, w_hh, b_ih, b_hh, out):
         keep = ctx.enter_context(tc.tile_pool(name="keep", bufs=1))
         stage = ctx.enter_context(tc.tile_pool(name="stage", bufs=2))
         quant = ctx.enter_context(tc.tile_pool(name="quant", bufs=3))
-        work = ctx.enter_context(tc.tile_pool(name="work", bufs=3))
+        work = ctx.enter_context(tc.tile_pool(name="work", bufs=4))
         psum = ctx.enter_context(tc.psum_pool(name="psum", bufs=1))
         ctx.enter_context(tc.manual_schedule())
 
@@ -50,106 +50,124 @@ def tile_grouptorchgru_kernel(tc, inputs, hidden, w_ih, w_hh, b_ih, b_hh, out):
         ident_f = keep.tile([P, P], F32, name="ident_f")
         masks.make_identity(nc, ident_f[:])
 
-        x_nat, w_nat, whh_nat, h_nat = [], [], [], []
-        for u in range(U):
-            x_nat.append(keep.tile([P, J, I], BF16, name="x_nat%d" % u))
-            nc.sync.dma_start(out=x_nat[u][:], in_=x_view[:, :, u * I:(u + 1) * I])
-            w_nat.append(keep.tile([P, GATES, I], BF16, name="w_nat%d" % u))
+        x_nat, w_nat, whh_nat, h_nat = {}, {}, {}, {}
+
+        def load_x(u, units):
+            tile = keep.tile([P, J, units * I], BF16, name="x_nat%d" % u)
+            nc.sync.dma_start(out=tile[:], in_=x_view[:, :, u * I:(u + units) * I])
+            for k in range(units):
+                x_nat[u + k] = tile[:, :, k * I:(k + 1) * I]
+
+        def load_hidden(u, units):
+            tile = keep.tile([P, J, units * H], BF16, name="h_nat%d" % u)
+            nc.sync.dma_start(out=tile[:], in_=h_view[:, :, u * H:(u + units) * H])
+            for k in range(units):
+                h_nat[u + k] = tile[:, :, k * H:(k + 1) * H]
+
+        def load_weights(u):
+            w_nat[u] = keep.tile([P, GATES, I], BF16, name="w_nat%d" % u)
             nc.sync.dma_start(out=w_nat[u][:], in_=w_view[:, u * GATES:(u + 1) * GATES, :])
-            if u % QUAD == 0:
-                h_nat.append(keep.tile([P, J, QUAD * H], BF16, name="h_nat%d" % (u // QUAD)))
-                nc.sync.dma_start(out=h_nat[u // QUAD][:], in_=h_view[:, :, u * H:(u + QUAD) * H])
-            whh_nat.append(keep.tile([P, GATES, H], BF16, name="whh_nat%d" % u))
+
+        def load_w_hh(u):
+            whh_nat[u] = keep.tile([P, GATES, H], BF16, name="whh_nat%d" % u)
             nc.sync.dma_start(out=whh_nat[u][:], in_=whh_view[:, u * GATES:(u + 1) * GATES, :])
 
-        def hidden_rows(u):
-            return h_nat[u // QUAD][:, :, (u % QUAD) * H:(u % QUAD + 1) * H]
+        for u in range(U):
+            load_x(u, 1)
+            load_weights(u)
+            if u in (0, 1):
+                load_hidden(u, 1)
+            if u == 2:
+                load_hidden(2, 2)
+            if u >= 4 and u % QUAD == 0:
+                load_hidden(u, QUAD)
+            load_w_hh(u)
 
-        bias_ps = psum.tile([P, J + GATES, P], BF16, tag="hidden_t", name="bias_ps")
-        nc.tensor.transpose(bias_ps[:, 0, :], bias_rows[:], ident_b[:])
+        def hidden_rows(u):
+            return h_nat[u]
+
         bias_cols = keep.tile([P, P], F32, name="bias_cols")
-        nc.vector.tensor_copy(out=bias_cols[:], in_=bias_ps[:, 0, :])
         bias_sum = keep.tile([P, U * GATES], F32, name="bias_sum")
-        nc.vector.tensor_tensor(out=bias_sum[:], in0=bias_cols[:, 0:U * GATES],
-                                in1=bias_cols[:, U * GATES:2 * U * GATES], op=ALU.add)
         bias_neg = keep.tile([P, U * GATES], F32, name="bias_neg")
-        nc.vector.tensor_scalar_mul(out=bias_neg[:], in0=bias_sum[:], scalar1=-1.0)
+
+        def transpose_biases():
+            bias_ps = psum.tile([P, P], BF16, tag="step_t", name="bias_ps")
+            nc.tensor.transpose(bias_ps[:], bias_rows[:], ident_b[:])
+            return bias_ps
+
+        def prepare_biases(bias_ps):
+            nc.vector.tensor_copy(out=bias_cols[:], in_=bias_ps[:])
+            nc.vector.tensor_tensor(out=bias_sum[:], in0=bias_cols[:, 0:U * GATES],
+                                    in1=bias_cols[:, U * GATES:2 * U * GATES], op=ALU.add)
+            nc.vector.tensor_scalar_mul(out=bias_neg[:], in0=bias_sum[:], scalar1=-1.0)
 
         def column(table, index):
             return table[:, index:index + 1]
 
         made = {}
 
-        def absent(u):
-            return u < 0 or u >= U
+        def bank(name, u, shape, dtype, tag):
+            if (name, u) not in made:
+                made[name, u] = psum.tile(shape, dtype, tag=tag, name=name)
+            return made[name, u]
 
-        def transpose_words(bank, rows):
-            for a in range(len(rows)):
-                for w in range(WORDS):
-                    nc.tensor.transpose(bank[:, a, w, :], rows[a].bitcast(F32)[:, w:WORDS * P:WORDS], ident_f[:])
+        def values(name, u, columns):
+            if (name, u) not in made:
+                made[name, u] = work.tile([P, columns], F32, name=name)
+            return made[name, u]
 
-        def interleave(copy, grouped, bank):
+        def transpose_words(ps, a, rows, words=range(WORDS)):
+            for w in words:
+                nc.tensor.transpose(ps[:, a, w, :], rows.bitcast(F32)[:, w:WORDS * P:WORDS], ident_f[:])
+
+        def interleave(copy, grouped, ps):
             copy(out=grouped.bitcast(F32).rearrange("p (a c w) -> p a c w", c=P, w=WORDS),
-                 in_=bank[:].rearrange("p a w c -> p a c w"))
+                 in_=ps[:].rearrange("p a w c -> p a c w"))
 
-        def transpose_x(u):
-            if absent(u):
-                return
-            made["x_t", u] = psum.tile([P, J, WORDS, P], F32, tag="x_t", name="x_t")
-            transpose_words(made["x_t", u], [x_nat[u][:, j, :] for j in range(J)])
+        def transpose_x(u, blocks=range(J)):
+            ps = bank("x_t", u, [P, J, WORDS, P], F32, "x_t")
+            for j in blocks:
+                transpose_words(ps, j, x_nat[u][:, j, :])
 
         def transpose_w_rz(u):
-            if absent(u):
-                return
-            made["w_rz_t", u] = psum.tile([P, 2, WORDS, P], F32, tag="w_rz_t", name="w_rz_t")
-            transpose_words(made["w_rz_t", u], [w_nat[u][:, g, :] for g in range(2)])
+            ps = bank("w_rz_t", u, [P, 2, WORDS, P], F32, "w_rz_t")
+            for g in range(2):
+                transpose_words(ps, g, w_nat[u][:, g, :])
 
-        def transpose_w_n(u):
-            if absent(u):
-                return
-            made["w_n_t", u] = psum.tile([P, 1, WORDS, P], F32, tag="w_n_t", name="w_n_t")
-            transpose_words(made["w_n_t", u], [w_nat[u][:, 2, :]])
+        def transpose_w_n(u, words=range(WORDS)):
+            transpose_words(bank("w_n_t", u, [P, 1, WORDS, P], F32, "w_n_t"), 0, w_nat[u][:, 2, :], words)
 
         def transpose_hidden(u):
-            if absent(u):
-                return
-            bank = psum.tile([P, J + GATES, P], BF16, tag="hidden_t", name="hidden_t")
+            ps = bank("hidden_t", u, [P, J + GATES, P], BF16, "hidden_t")
             for j in range(J):
-                nc.tensor.transpose(bank[:, j, :], hidden_rows(u)[:, j, :], ident_b[:])
+                nc.tensor.transpose(ps[:, j, :], hidden_rows(u)[:, j, :], ident_b[:])
             for g in range(GATES):
-                nc.tensor.transpose(bank[:, J + g, :], whh_nat[u][:, g, :], ident_b[:])
-            made["hidden_t", u] = bank
+                nc.tensor.transpose(ps[:, J + g, :], whh_nat[u][:, g, :], ident_b[:])
 
         def copy_x(u):
-            if absent(u):
-                return
             made["x_w_rz", u] = stage.tile([P, (B + 2 * H) * PACK], BF16, name="x_w_rz", align_bytes=64)
             interleave(nc.scalar.copy, made["x_w_rz", u][:, 0:B * PACK], made["x_t", u])
 
-        def copy_w_rz(u):
-            if absent(u):
-                return
-            interleave(nc.scalar.copy, made["x_w_rz", u][:, B * PACK:(B + 2 * H) * PACK], made["w_rz_t", u])
+        def copy_w_rz(u, copy=nc.scalar.copy):
+            interleave(copy, made["x_w_rz", u][:, B * PACK:(B + 2 * H) * PACK], made["w_rz_t", u])
 
         def copy_w_n(u):
-            if absent(u):
-                return
             made["w_n", u] = stage.tile([P, H * PACK], BF16, name="w_n", align_bytes=64)
-            interleave(nc.vector.tensor_copy, made["w_n", u][:], made["w_n_t", u])
+            interleave(nc.scalar.copy if u == U - 1 else nc.vector.tensor_copy, made["w_n", u][:], made["w_n_t", u])
 
         def copy_hidden(u):
-            if absent(u):
-                return
-            made["hidden", u] = keep.tile([P, J + GATES, P], BF16, name="hidden%d" % u)
-            copy = nc.scalar.copy if u % 2 == 0 else nc.vector.tensor_copy
-            copy(out=made["hidden", u][:], in_=made["hidden_t", u][:])
+            made["hidden", u] = keep.tile([P, J, P], BF16, name="hidden%d" % u)
+            nc.scalar.copy(out=made["hidden", u][:], in_=made["hidden_t", u][:, 0:J, :])
+
+        def copy_w_hh(u):
+            made["w_hh", u] = keep.tile([P, GATES, P], BF16, name="w_hh%d" % u)
+            copy = nc.scalar.copy if u == U - 1 else nc.vector.tensor_copy
+            copy(out=made["w_hh", u][:], in_=made["hidden_t", u][:, J:J + GATES, :])
 
         def hidden_t(u):
-            return made["hidden", u][:, 0:J, :].rearrange("p j b -> p (j b)")
+            return made["hidden", u][:].rearrange("p j b -> p (j b)")
 
         def quantise(u, name):
-            if absent(u):
-                return
             columns = made[name, u].shape[1] // PACK
             codes = quant.tile([P, columns], U32, name=name + "_codes", align_bytes=64)
             scales = quant.tile([P, columns], U8, name=name + "_scales", align_bytes=64)
@@ -166,130 +184,189 @@ def tile_grouptorchgru_kernel(tc, inputs, hidden, w_ih, w_hh, b_ih, b_hh, out):
                                 start=True, stop=True)
 
         def matmul_h(u, acc, g):
-            nc.tensor.matmul(out=acc, lhsT=made["hidden", u][:, J + g, :], rhs=hidden_t(u), start=True, stop=True)
+            nc.tensor.matmul(out=acc, lhsT=made["w_hh", u][:, g, :], rhs=hidden_t(u), start=True, stop=True)
 
-        def matmul_h_rz(u):
-            if absent(u):
-                return
-            made["h_rz", u] = psum.tile([P, 2 * B], F32, tag="h_rz", name="h_rz")
-            for g in range(2):
-                matmul_h(u, made["h_rz", u][:, g * B:(g + 1) * B], g)
+        def matmul_h_rz(u, g):
+            ps = bank("h_rz", u, [P, 2 * B], F32, "w_rz_t" if u == U - 1 else "h_rz")
+            matmul_h(u, ps[:, g * B:(g + 1) * B], g)
 
-        def matmul_x_rz(u):
-            if absent(u):
-                return
-            made["x_rz", u] = psum.tile([P, 2 * B], F32, tag="x_rz", name="x_rz")
-            for g in range(2):
-                matmul_x(u, made["x_rz", u][:, g * B:(g + 1) * B], made["x_w_rz_q", u], B + g * H)
+        def matmul_x_rz(u, g):
+            ps = bank("x_rz", u, [P, 2 * B], F32, "x_t" if u == U - 1 else "x_rz")
+            matmul_x(u, ps[:, g * B:(g + 1) * B], made["x_w_rz_q", u], B + g * H)
 
-        def matmul_n(u):
-            if absent(u):
-                return
-            made["hx_n", u] = psum.tile([P, 2 * B], F32, tag="hx_n", name="hx_n")
-            matmul_h(u, made["hx_n", u][:, 0:B], 2)
-            matmul_x(u, made["hx_n", u][:, B:2 * B], made["w_n_q", u], 0)
+        def hx_n_tag(u):
+            return {U - 2: "h_rz", U - 1: "w_n_t"}.get(u, "hx_n")
+
+        def matmul_h_n(u):
+            matmul_h(u, bank("hx_n", u, [P, 2 * B], F32, hx_n_tag(u))[:, 0:B], 2)
+
+        def matmul_x_n(u):
+            ps = bank("hx_n", u, [P, 2 * B], F32, hx_n_tag(u))
+            matmul_x(u, ps[:, B:2 * B], made["w_n_q", u], 0)
 
         def copy_h_rz(u):
-            if absent(u):
-                return
-            made["h_rz_sb", u] = work.tile([P, 2 * B], F32, name="h_rz_sb")
-            nc.scalar.copy(out=made["h_rz_sb", u][:], in_=made["h_rz", u][:])
+            nc.scalar.copy(out=values("h_rz_sb", u, 2 * B)[:], in_=made["h_rz", u][:])
 
-        def add_rz(u):
-            if absent(u):
-                return
-            made["rz", u] = work.tile([P, 2 * B], F32, name="rz")
-            nc.vector.tensor_tensor(out=made["rz", u][:], in0=made["x_rz", u][:], in1=made["h_rz_sb", u][:],
-                                    op=ALU.add)
+        def add_rz(u, first=0, last=2 * B):
+            nc.vector.tensor_tensor(out=values("rz", u, 2 * B)[:, first:last], in0=made["x_rz", u][:, first:last],
+                                    in1=made["h_rz_sb", u][:, first:last], op=ALU.add)
 
-        def reset_gate(u):
-            if absent(u):
-                return
-            made["r", u] = work.tile([P, B], F32, name="r")
-            nc.scalar.activation(out=made["r", u][:], in_=made["rz", u][:, 0:B], func=ACT.Sigmoid,
-                                 bias=column(bias_sum, u * GATES), scale=1.0)
+        def reset_gate(u, first=0, last=B):
+            nc.scalar.activation(out=values("r", u, B)[:, first:last], in_=made["rz", u][:, first:last],
+                                 func=ACT.Sigmoid, bias=column(bias_sum, u * GATES), scale=1.0)
 
         def update_gate(u):
-            if absent(u):
-                return
-            made["one_minus_z", u] = work.tile([P, B], F32, name="one_minus_z")
-            nc.scalar.activation(out=made["one_minus_z", u][:], in_=made["rz", u][:, B:2 * B], func=ACT.Sigmoid,
-                                 bias=column(bias_neg, u * GATES + 1), scale=-1.0)
+            nc.scalar.activation(out=values("one_minus_z", u, B)[:], in_=made["rz", u][:, B:2 * B],
+                                 func=ACT.Sigmoid, bias=column(bias_neg, u * GATES + 1), scale=-1.0)
 
-        def reset_times_hn(u):
-            if absent(u):
-                return
-            made["r_hn", u] = work.tile([P, B], F32, name="r_hn")
-            nc.vector.scalar_tensor_tensor(out=made["r_hn", u][:], in0=made["hx_n", u][:, 0:B],
-                                           scalar=column(bias_cols, (U + u) * GATES + 2), in1=made["r", u][:],
-                                           op0=ALU.add, op1=ALU.mult)
+        def reset_times_hn(u, first=0, last=B):
+            nc.vector.scalar_tensor_tensor(out=values("r_hn", u, B)[:, first:last], in0=made["hx_n", u][:, first:last],
+                                           scalar=column(bias_cols, (U + u) * GATES + 2),
+                                           in1=made["r", u][:, first:last], op0=ALU.add, op1=ALU.mult)
 
-        def add_xn(u):
-            if absent(u):
-                return
-            made["n_sum", u] = work.tile([P, B], F32, name="n_sum")
-            nc.vector.tensor_tensor(out=made["n_sum", u][:], in0=made["hx_n", u][:, B:2 * B],
-                                    in1=made["r_hn", u][:], op=ALU.add)
+        def add_xn(u, first=0, last=B):
+            nc.vector.tensor_tensor(out=values("n_sum", u, B)[:, first:last], in0=made["hx_n", u][:, B + first:B + last],
+                                    in1=made["r_hn", u][:, first:last], op=ALU.add)
 
-        def new_gate(u):
-            if absent(u):
-                return
-            made["n", u] = work.tile([P, B], F32, name="n")
-            nc.scalar.activation(out=made["n", u][:], in_=made["n_sum", u][:], func=ACT.Tanh,
-                                 bias=column(bias_cols, u * GATES + 2), scale=1.0)
+        def new_gate(u, first=0, last=B):
+            nc.scalar.activation(out=values("n", u, B)[:, first:last], in_=made["n_sum", u][:, first:last],
+                                 func=ACT.Tanh, bias=column(bias_cols, u * GATES + 2), scale=1.0)
 
-        def blend(u):
-            if absent(u):
-                return
-            engine = nc.gpsimd if u < U - 2 else nc.vector
-            made["n_minus_h", u] = work.tile([P, B], F32, name="n_minus_h")
-            engine.tensor_tensor(out=made["n_minus_h", u][:], in0=made["n", u][:], in1=hidden_t(u), op=ALU.subtract)
-            made["step", u] = work.tile([P, B], F32, name="step")
-            engine.tensor_tensor(out=made["step", u][:], in0=made["one_minus_z", u][:], in1=made["n_minus_h", u][:],
-                                 op=ALU.mult)
+        def subtract_hidden(u, engine, first=0, last=B):
+            engine.tensor_tensor(out=values("n_minus_h", u, B)[:, first:last], in0=made["n", u][:, first:last],
+                                 in1=hidden_t(u)[:, first:last], op=ALU.subtract)
 
-        def transpose_back(u):
-            if absent(u):
-                return
-            made["step_t", u] = psum.tile([P, J, H], F32, tag="step_t", name="step_t")
-            for j in range(J):
-                nc.tensor.transpose(made["step_t", u][:, j, :], made["step", u][:, j * P:(j + 1) * P], ident_f[:])
+        def times_update(u, engine, first=0, last=B):
+            engine.tensor_tensor(out=values("step", u, B)[:, first:last], in0=made["one_minus_z", u][:, first:last],
+                                 in1=made["n_minus_h", u][:, first:last], op=ALU.mult)
+
+        def blend(u, engine):
+            subtract_hidden(u, engine)
+            times_update(u, engine)
+
+        def transpose_back(u, blocks=range(J)):
+            ps = bank("step_t", u, [P, J, H], F32, {U - 3: "hidden_t", U - 2: "hx_n", U - 1: "x_rz"}.get(u, "step_t"))
+            for j in blocks:
+                nc.tensor.transpose(ps[:, j, :], made["step", u][:, j * P:(j + 1) * P], ident_f[:])
+
+        def add_hidden(u, first=0, last=J):
+            if ("out", u // 2) not in made:
+                made["out", u // 2] = keep.tile([P, J, 2 * H], F32, name="out%d" % (u // 2))
+            nc.vector.tensor_tensor(out=made["out", u // 2][:, first:last, (u % 2) * H:(u % 2 + 1) * H],
+                                    in0=made["step_t", u][:, first:last, :], in1=hidden_rows(u)[:, first:last, :],
+                                    op=ALU.add)
+
+        def store_pair(u):
+            nc.sync.dma_start(out=out_view[:, :, (u - 1) * H:(u + 1) * H], in_=made["out", u // 2][:])
 
         def add_hidden_and_store(u):
-            if absent(u):
-                return
-            if u % 2 == 0:
-                made["out", u // 2] = keep.tile([P, J, 2 * H], F32, name="out%d" % (u // 2))
-            pair = made["out", u // 2]
-            nc.vector.tensor_tensor(out=pair[:, :, (u % 2) * H:(u % 2 + 1) * H], in0=made["step_t", u][:],
-                                    in1=hidden_rows(u), op=ALU.add)
+            add_hidden(u)
             if u % 2 == 1:
-                nc.sync.dma_start(out=out_view[:, :, (u - 1) * H:(u + 1) * H], in_=pair[:])
+                store_pair(u)
 
-        for i in range(-2, U + 3):
-            copy_x(i + 1)
-            copy_w_rz(i + 1)
-            copy_h_rz(i)
-            reset_gate(i - 1)
-            new_gate(i - 2)
-            copy_w_n(i + 1)
-            copy_hidden(i + 1)
-            update_gate(i - 2)
+        def run(step, u, *rest):
+            if 0 <= u < U:
+                step(u, *rest)
 
-            matmul_n(i - 1)
-            transpose_x(i + 2)
-            transpose_w_rz(i + 2)
-            transpose_back(i - 3)
+        for i in range(-2, U - 2):
+            run(copy_w_n, i + 1)
+            run(copy_w_hh, i + 1)
+            run(copy_x, i + 1)
+            run(copy_w_rz, i + 1)
+            run(copy_h_rz, i)
+            run(reset_gate, i - 1)
+            run(new_gate, i - 2)
+            run(copy_hidden, i + 1)
+            run(update_gate, i - 2)
 
-            quantise(i + 1, "x_w_rz")
-            quantise(i + 1, "w_n")
-            reset_times_hn(i - 1)
-            add_rz(i)
-            add_xn(i - 1)
-            blend(i - 2)
-            add_hidden_and_store(i - 3)
+            run(matmul_x_n, i - 1)
+            run(transpose_x, i + 2, (0,))
+            run(matmul_h_n, i - 1)
+            run(transpose_x, i + 2, (1,))
+            run(transpose_w_rz, i + 2)
+            run(transpose_back, i - 3)
 
-            matmul_h_rz(i + 1)
-            transpose_w_n(i + 2)
-            transpose_hidden(i + 2)
-            matmul_x_rz(i + 1)
+            run(quantise, i + 1, "x_w_rz")
+            run(add_rz, i)
+            run(reset_times_hn, i - 1)
+            run(quantise, i + 1, "w_n")
+            run(add_xn, i - 1)
+            run(add_hidden_and_store, i - 3)
+            run(blend, i - 2, nc.gpsimd)
+
+            run(matmul_h_rz, i + 1, 0)
+            run(transpose_w_n, i + 2, (0,))
+            run(matmul_h_rz, i + 1, 1)
+            run(transpose_w_n, i + 2, (1,))
+            run(transpose_hidden, i + 2)
+            run(matmul_x_rz, i + 1, 0)
+            run(matmul_x_rz, i + 1, 1)
+            if i == -2:
+                bias_ps = transpose_biases()
+            elif i == -1:
+                prepare_biases(bias_ps)
+
+        z, a, b, c, d = range(U - 5, U)
+        halves = [(j * P, (j + 1) * P) for j in range(J)]
+        copy_x(d)
+        copy_w_rz(d)
+        copy_h_rz(c)
+        copy_hidden(d)
+        copy_w_hh(d)
+        reset_gate(b)
+        copy_w_n(d)
+        new_gate(a)
+        matmul_h_n(b)
+        matmul_x_n(b)
+        transpose_back(z)
+        matmul_h_n(c)
+        matmul_x_n(c)
+        matmul_h_rz(d, 0)
+        matmul_h_rz(d, 1)
+        quantise(d, "x_w_rz")
+        matmul_x_rz(d, 0)
+        matmul_x_rz(d, 1)
+        add_rz(c)
+        reset_gate(c)
+        copy_h_rz(d)
+        reset_times_hn(b)
+        quantise(d, "w_n")
+        add_xn(b)
+        update_gate(a)
+        new_gate(b)
+        update_gate(b)
+        add_hidden_and_store(z)
+        reset_times_hn(c)
+        matmul_x_n(d)
+        matmul_h_n(d)
+        add_rz(d, 0, B)
+        blend(a, nc.gpsimd)
+        for first, last in halves:
+            reset_gate(d, first, last)
+        add_xn(c)
+        add_rz(d, B, 2 * B)
+        new_gate(c)
+        update_gate(c)
+        update_gate(d)
+        transpose_back(a)
+        blend(b, nc.gpsimd)
+        for first, last in halves:
+            reset_times_hn(d, first, last)
+        for first, last in halves:
+            add_xn(d, first, last)
+            new_gate(d, first, last)
+        subtract_hidden(c, nc.vector)
+        add_hidden_and_store(a)
+        times_update(c, nc.vector)
+        transpose_back(b)
+        transpose_back(c)
+        for first, last in halves:
+            subtract_hidden(d, nc.vector, first, last)
+        add_hidden_and_store(b)
+        for j, (first, last) in enumerate(halves):
+            times_update(d, nc.vector, first, last)
+            transpose_back(d, (j,))
+        add_hidden(c)
+        for j in range(J):
+            add_hidden(d, j, j + 1)
+        store_pair(d)

@@ -280,9 +280,8 @@ def tile_grouptorchgru_kernel(tc, inputs, hidden, w_ih, w_hh, b_ih, b_hh, out):
             run(update_gate, i - 2)
 
             run(matmul_x_n, i - 1)
-            run(transpose_x, i + 2, (0,))
             run(matmul_h_n, i - 1)
-            run(transpose_x, i + 2, (1,))
+            run(transpose_x, i + 2)
             run(transpose_w_rz, i + 2)
             run(transpose_back, i - 3)
 
@@ -295,9 +294,8 @@ def tile_grouptorchgru_kernel(tc, inputs, hidden, w_ih, w_hh, b_ih, b_hh, out):
             run(blend, i - 2, nc.gpsimd)
 
             run(matmul_h_rz, i + 1, 0)
-            run(transpose_w_n, i + 2, (0,))
             run(matmul_h_rz, i + 1, 1)
-            run(transpose_w_n, i + 2, (1,))
+            run(transpose_w_n, i + 2)
             run(transpose_hidden, i + 2)
             run(matmul_x_rz, i + 1, 0)
             run(matmul_x_rz, i + 1, 1)

@@ -18,6 +18,7 @@ GATES = 3
 PACK = 4
 WORDS = PACK // 2
 QUAD = 4
+WARM = 6
 FLOPS = 2 * B * U * GATES * H * (I + H)
 
 
@@ -50,6 +51,12 @@ def tile_grouptorchgru_kernel(tc, inputs, hidden, w_ih, w_hh, b_ih, b_hh, out):
         ident_f = keep.tile([P, P], F32, name="ident_f")
         masks.make_identity(nc, ident_f[:])
 
+        ones = keep.tile([P, B], BF16, name="ones")
+        nc.vector.memset(ones[:], 1.0)
+        warm_ps = psum.tile([P, B], F32, tag="hx_n", name="warm_ps")
+        for k in range(WARM):
+            nc.tensor.matmul(out=warm_ps[:], lhsT=ones[:, 0:P], rhs=ones[:], start=True, stop=True)
+
         x_nat, w_nat, whh_nat, h_nat = {}, {}, {}, {}
 
         def load_x(u, units):
@@ -66,7 +73,9 @@ def tile_grouptorchgru_kernel(tc, inputs, hidden, w_ih, w_hh, b_ih, b_hh, out):
 
         def load_weights(u):
             w_nat[u] = keep.tile([P, GATES, I], BF16, name="w_nat%d" % u)
-            nc.sync.dma_start(out=w_nat[u][:], in_=w_view[:, u * GATES:(u + 1) * GATES, :])
+            nc.sync.dma_start(out=w_nat[u][:, 0:2, :].rearrange("p a k -> p (a k)"),
+                              in_=w_ih[u, 0:2 * P, :].rearrange("(p a) k -> p (a k)", a=2))
+            nc.sync.dma_start(out=w_nat[u][:, 2, :], in_=w_ih[u, 2 * P:GATES * P, :])
 
         def load_w_hh(u):
             whh_nat[u] = keep.tile([P, GATES, H], BF16, name="whh_nat%d" % u)
@@ -149,7 +158,9 @@ def tile_grouptorchgru_kernel(tc, inputs, hidden, w_ih, w_hh, b_ih, b_hh, out):
             interleave(nc.scalar.copy, made["x_w_rz", u][:, 0:B * PACK], made["x_t", u])
 
         def copy_w_rz(u, copy=nc.scalar.copy):
-            interleave(copy, made["x_w_rz", u][:, B * PACK:(B + 2 * H) * PACK], made["w_rz_t", u])
+            copy(out=made["x_w_rz", u][:, B * PACK:(B + 2 * H) * PACK].bitcast(F32).rearrange(
+                     "p (c a w) -> p c a w", a=2, w=WORDS),
+                 in_=made["w_rz_t", u][:].rearrange("p a w c -> p c a w"))
 
         def copy_w_n(u):
             made["w_n", u] = stage.tile([P, H * PACK], BF16, name="w_n", align_bytes=64)
@@ -259,6 +270,10 @@ def tile_grouptorchgru_kernel(tc, inputs, hidden, w_ih, w_hh, b_ih, b_hh, out):
         def store_pair(u):
             nc.sync.dma_start(out=out_view[:, :, (u - 1) * H:(u + 1) * H], in_=made["out", u // 2][:])
 
+        def store(u, first=0, last=J):
+            nc.sync.dma_start(out=out_view[:, first:last, u * H:(u + 1) * H],
+                              in_=made["out", u // 2][:, first:last, (u % 2) * H:(u % 2 + 1) * H])
+
         def add_hidden_and_store(u):
             add_hidden(u)
             if u % 2 == 1:
@@ -365,6 +380,7 @@ def tile_grouptorchgru_kernel(tc, inputs, hidden, w_ih, w_hh, b_ih, b_hh, out):
             times_update(d, nc.vector, first, last)
             transpose_back(d, (j,))
         add_hidden(c)
+        store(c)
         for j in range(J):
             add_hidden(d, j, j + 1)
-        store_pair(d)
+            store(d, j, j + 1)

@@ -39,9 +39,6 @@ def tile_grouptorchgru_kernel(tc, inputs, hidden, w_ih, w_hh, b_ih, b_hh, out):
         ctx.enter_context(tc.manual_schedule())
 
         bias_rows = keep.tile([P, P], BF16, name="bias_rows")
-        nc.scalar.dma_start(out=bias_rows[0:U * GATES, :], in_=b_ih.rearrange("u (g h) -> (u g) h", h=H))
-        nc.scalar.dma_start(out=bias_rows[U * GATES:2 * U * GATES, :],
-                            in_=b_hh.rearrange("u (g h) -> (u g) h", h=H))
         nc.vector.memset(bias_rows[2 * U * GATES:P, :], 0.0)
         warm = keep.tile([P, 2], F32, name="warm")
         nc.vector.memset(warm[:], 0.0)
@@ -50,6 +47,9 @@ def tile_grouptorchgru_kernel(tc, inputs, hidden, w_ih, w_hh, b_ih, b_hh, out):
         masks.make_identity(nc, ident_b[:])
         ident_f = keep.tile([P, P], F32, name="ident_f")
         masks.make_identity(nc, ident_f[:])
+        nc.gpsimd.dma_start(out=bias_rows[0:U * GATES, :], in_=b_ih.rearrange("u (g h) -> (u g) h", h=H))
+        nc.gpsimd.dma_start(out=bias_rows[U * GATES:2 * U * GATES, :],
+                            in_=b_hh.rearrange("u (g h) -> (u g) h", h=H))
 
         ones = keep.tile([P, B], BF16, name="ones")
         nc.vector.memset(ones[:], 1.0)
@@ -143,15 +143,24 @@ def tile_grouptorchgru_kernel(tc, inputs, hidden, w_ih, w_hh, b_ih, b_hh, out):
             for g in range(2):
                 transpose_words(ps, g, w_nat[u][:, g, :])
 
-        def transpose_w_n(u, words=range(WORDS)):
-            transpose_words(bank("w_n_t", u, [P, 1, WORDS, P], F32, "w_n_t"), 0, w_nat[u][:, 2, :], words)
+        def transpose_w_n(u):
+            ps = bank("w_n_t", u, [P, WORDS * P + GATES * P // 2], F32, "w_n_t")
+            for w in range(WORDS):
+                nc.tensor.transpose(ps[:, w * P:(w + 1) * P], w_nat[u][:, 2, :].bitcast(F32)[:, w:WORDS * P:WORDS],
+                                    ident_f[:])
+
+        def transpose_w_hh(u):
+            ps = w_hh_t(u)
+            for g in range(GATES):
+                nc.tensor.transpose(ps[:, g * P:(g + 1) * P], whh_nat[u][:, g, :], ident_b[:])
+
+        def w_hh_t(u):
+            return made["w_n_t", u][:, WORDS * P:WORDS * P + GATES * P // 2].bitcast(BF16)
 
         def transpose_hidden(u):
-            ps = bank("hidden_t", u, [P, J + GATES, P], BF16, "hidden_t")
+            ps = bank("hidden_t", u, [P, J, P], BF16, "hidden_t")
             for j in range(J):
                 nc.tensor.transpose(ps[:, j, :], hidden_rows(u)[:, j, :], ident_b[:])
-            for g in range(GATES):
-                nc.tensor.transpose(ps[:, J + g, :], whh_nat[u][:, g, :], ident_b[:])
 
         def copy_x(u):
             made["x_w_rz", u] = stage.tile([P, (B + 2 * H) * PACK], BF16, name="x_w_rz", align_bytes=64)
@@ -164,16 +173,18 @@ def tile_grouptorchgru_kernel(tc, inputs, hidden, w_ih, w_hh, b_ih, b_hh, out):
 
         def copy_w_n(u):
             made["w_n", u] = stage.tile([P, H * PACK], BF16, name="w_n", align_bytes=64)
-            interleave(nc.scalar.copy if u == U - 1 else nc.vector.tensor_copy, made["w_n", u][:], made["w_n_t", u])
+            copy = nc.scalar.copy if u == U - 1 else nc.vector.tensor_copy
+            copy(out=made["w_n", u][:].bitcast(F32).rearrange("p (c w) -> p c w", w=WORDS),
+                 in_=made["w_n_t", u][:, 0:WORDS * P].rearrange("p (w c) -> p c w", w=WORDS))
 
         def copy_hidden(u):
             made["hidden", u] = keep.tile([P, J, P], BF16, name="hidden%d" % u)
-            nc.scalar.copy(out=made["hidden", u][:], in_=made["hidden_t", u][:, 0:J, :])
+            nc.scalar.copy(out=made["hidden", u][:], in_=made["hidden_t", u][:])
 
         def copy_w_hh(u):
-            made["w_hh", u] = keep.tile([P, GATES, P], BF16, name="w_hh%d" % u)
+            made["w_hh", u] = keep.tile([P, GATES * P], BF16, name="w_hh%d" % u)
             copy = nc.scalar.copy if u == U - 1 else nc.vector.tensor_copy
-            copy(out=made["w_hh", u][:], in_=made["hidden_t", u][:, J:J + GATES, :])
+            copy(out=made["w_hh", u][:], in_=w_hh_t(u))
 
         def hidden_t(u):
             return made["hidden", u][:].rearrange("p j b -> p (j b)")
@@ -195,7 +206,7 @@ def tile_grouptorchgru_kernel(tc, inputs, hidden, w_ih, w_hh, b_ih, b_hh, out):
                                 start=True, stop=True)
 
         def matmul_h(u, acc, g):
-            nc.tensor.matmul(out=acc, lhsT=made["w_hh", u][:, g, :], rhs=hidden_t(u), start=True, stop=True)
+            nc.tensor.matmul(out=acc, lhsT=made["w_hh", u][:, g * P:(g + 1) * P], rhs=hidden_t(u), start=True, stop=True)
 
         def matmul_h_rz(u, g):
             ps = bank("h_rz", u, [P, 2 * B], F32, "w_rz_t" if u == U - 1 else "h_rz")
@@ -311,12 +322,13 @@ def tile_grouptorchgru_kernel(tc, inputs, hidden, w_ih, w_hh, b_ih, b_hh, out):
             run(matmul_h_rz, i + 1, 0)
             run(matmul_h_rz, i + 1, 1)
             run(transpose_w_n, i + 2)
+            run(transpose_w_hh, i + 2)
             run(transpose_hidden, i + 2)
             run(matmul_x_rz, i + 1, 0)
             run(matmul_x_rz, i + 1, 1)
-            if i == -2:
+            if i == -1:
                 bias_ps = transpose_biases()
-            elif i == -1:
+            elif i == 0:
                 prepare_biases(bias_ps)
 
         z, a, b, c, d = range(U - 5, U)
@@ -362,13 +374,14 @@ def tile_grouptorchgru_kernel(tc, inputs, hidden, w_ih, w_hh, b_ih, b_hh, out):
         update_gate(c)
         update_gate(d)
         transpose_back(a)
-        blend(b, nc.gpsimd)
+        subtract_hidden(b, nc.gpsimd)
         for first, last in halves:
             reset_times_hn(d, first, last)
         for first, last in halves:
             add_xn(d, first, last)
             new_gate(d, first, last)
         subtract_hidden(c, nc.vector)
+        times_update(b, nc.vector)
         add_hidden_and_store(a)
         times_update(c, nc.vector)
         transpose_back(b)

from contextlib import ExitStack

import concourse.masks as masks
import concourse.mybir as mybir

F32 = mybir.dt.float32
BF16 = mybir.dt.bfloat16
U32 = mybir.dt.uint32
U8 = mybir.dt.uint8
FP8X4 = mybir.dt.float8_e4m3fn_x4
ACT = mybir.ActivationFunctionType
ALU = mybir.AluOpType

P = 128
B, U, I, H = 256, 16, 512, 128
J = B // P
GATES = 3
PACK = 4
WORDS = PACK // 2
QUAD = 4
WARM = 6
FLOPS = 2 * B * U * GATES * H * (I + H)


def tile_grouptorchgru_kernel(tc, inputs, hidden, w_ih, w_hh, b_ih, b_hh, out):
    nc = tc.nc
    x_view = inputs.rearrange("(j p) u k -> p j (u k)", p=P)
    h_view = hidden.rearrange("(j p) u h -> p j (u h)", p=P)
    out_view = out.rearrange("(j p) u h -> p j (u h)", p=P)
    w_view = w_ih.flatten_outer_dims().rearrange("(g p) k -> p g k", p=P)
    whh_view = w_hh.flatten_outer_dims().rearrange("(g p) k -> p g k", p=P)

    with ExitStack() as ctx:
        keep = ctx.enter_context(tc.tile_pool(name="keep", bufs=1))
        stage = ctx.enter_context(tc.tile_pool(name="stage", bufs=2))
        quant = ctx.enter_context(tc.tile_pool(name="quant", bufs=3))
        work = ctx.enter_context(tc.tile_pool(name="work", bufs=4))
        psum = ctx.enter_context(tc.psum_pool(name="psum", bufs=1))
        ctx.enter_context(tc.manual_schedule())

        bias_rows = keep.tile([P, P], BF16, name="bias_rows")
        nc.vector.memset(bias_rows[2 * U * GATES:P, :], 0.0)
        warm = keep.tile([P, 2], F32, name="warm")
        nc.vector.memset(warm[:], 0.0)
        nc.scalar.activation(out=warm[:, 1:2], in_=warm[:, 0:1], func=ACT.Sigmoid)
        ident_b = keep.tile([P, P], BF16, name="ident_b")
        masks.make_identity(nc, ident_b[:])
        ident_f = keep.tile([P, P], F32, name="ident_f")
        masks.make_identity(nc, ident_f[:])
        nc.gpsimd.dma_start(out=bias_rows[0:U * GATES, :], in_=b_ih.rearrange("u (g h) -> (u g) h", h=H))
        nc.gpsimd.dma_start(out=bias_rows[U * GATES:2 * U * GATES, :],
                            in_=b_hh.rearrange("u (g h) -> (u g) h", h=H))

        ones = keep.tile([P, B], BF16, name="ones")
        nc.vector.memset(ones[:], 1.0)
        warm_ps = psum.tile([P, B], F32, tag="hx_n", name="warm_ps")
        for k in range(WARM):
            nc.tensor.matmul(out=warm_ps[:], lhsT=ones[:, 0:P], rhs=ones[:], start=True, stop=True)

        x_nat, w_nat, whh_nat, h_nat = {}, {}, {}, {}

        def load_x(u, units):
            tile = keep.tile([P, J, units * I], BF16, name="x_nat%d" % u)
            nc.sync.dma_start(out=tile[:], in_=x_view[:, :, u * I:(u + units) * I])
            for k in range(units):
                x_nat[u + k] = tile[:, :, k * I:(k + 1) * I]

        def load_hidden(u, units):
            tile = keep.tile([P, J, units * H], BF16, name="h_nat%d" % u)
            nc.sync.dma_start(out=tile[:], in_=h_view[:, :, u * H:(u + units) * H])
            for k in range(units):
                h_nat[u + k] = tile[:, :, k * H:(k + 1) * H]

        def load_weights(u):
            w_nat[u] = keep.tile([P, GATES, I], BF16, name="w_nat%d" % u)
            nc.sync.dma_start(out=w_nat[u][:, 0:2, :].rearrange("p a k -> p (a k)"),
                              in_=w_ih[u, 0:2 * P, :].rearrange("(p a) k -> p (a k)", a=2))
            nc.sync.dma_start(out=w_nat[u][:, 2, :], in_=w_ih[u, 2 * P:GATES * P, :])

        def load_w_hh(u):
            whh_nat[u] = keep.tile([P, GATES, H], BF16, name="whh_nat%d" % u)
            nc.sync.dma_start(out=whh_nat[u][:], in_=whh_view[:, u * GATES:(u + 1) * GATES, :])

        for u in range(U):
            load_x(u, 1)
            load_weights(u)
            if u in (0, 1):
                load_hidden(u, 1)
            if u == 2:
                load_hidden(2, 2)
            if u >= 4 and u % QUAD == 0:
                load_hidden(u, QUAD)
            load_w_hh(u)

        def hidden_rows(u):
            return h_nat[u]

        bias_cols = keep.tile([P, P], F32, name="bias_cols")
        bias_sum = keep.tile([P, U * GATES], F32, name="bias_sum")
        bias_neg = keep.tile([P, U * GATES], F32, name="bias_neg")

        def transpose_biases():
            bias_ps = psum.tile([P, P], BF16, tag="step_t", name="bias_ps")
            nc.tensor.transpose(bias_ps[:], bias_rows[:], ident_b[:])
            return bias_ps

        def prepare_biases(bias_ps):
            nc.vector.tensor_copy(out=bias_cols[:], in_=bias_ps[:])
            nc.vector.tensor_tensor(out=bias_sum[:], in0=bias_cols[:, 0:U * GATES],
                                    in1=bias_cols[:, U * GATES:2 * U * GATES], op=ALU.add)
            nc.vector.tensor_scalar_mul(out=bias_neg[:], in0=bias_sum[:], scalar1=-1.0)

        def column(table, index):
            return table[:, index:index + 1]

        made = {}

        def bank(name, u, shape, dtype, tag):
            if (name, u) not in made:
                made[name, u] = psum.tile(shape, dtype, tag=tag, name=name)
            return made[name, u]

        def values(name, u, columns):
            if (name, u) not in made:
                made[name, u] = work.tile([P, columns], F32, name=name)
            return made[name, u]

        def transpose_words(ps, a, rows, words=range(WORDS)):
            for w in words:
                nc.tensor.transpose(ps[:, a, w, :], rows.bitcast(F32)[:, w:WORDS * P:WORDS], ident_f[:])

        def interleave(copy, grouped, ps):
            copy(out=grouped.bitcast(F32).rearrange("p (a c w) -> p a c w", c=P, w=WORDS),
                 in_=ps[:].rearrange("p a w c -> p a c w"))

        def transpose_x(u, blocks=range(J)):
            ps = bank("x_t", u, [P, J, WORDS, P], F32, "x_t")
            for j in blocks:
                transpose_words(ps, j, x_nat[u][:, j, :])

        def transpose_w_rz(u):
            ps = bank("w_rz_t", u, [P, 2, WORDS, P], F32, "w_rz_t")
            for g in range(2):
                transpose_words(ps, g, w_nat[u][:, g, :])

        def transpose_w_n(u):
            ps = bank("w_n_t", u, [P, WORDS * P + GATES * P // 2], F32, "w_n_t")
            for w in range(WORDS):
                nc.tensor.transpose(ps[:, w * P:(w + 1) * P], w_nat[u][:, 2, :].bitcast(F32)[:, w:WORDS * P:WORDS],
                                    ident_f[:])

        def transpose_w_hh(u):
            ps = w_hh_t(u)
            for g in range(GATES):
                nc.tensor.transpose(ps[:, g * P:(g + 1) * P], whh_nat[u][:, g, :], ident_b[:])

        def w_hh_t(u):
            return made["w_n_t", u][:, WORDS * P:WORDS * P + GATES * P // 2].bitcast(BF16)

        def transpose_hidden(u):
            ps = bank("hidden_t", u, [P, J, P], BF16, "hidden_t")
            for j in range(J):
                nc.tensor.transpose(ps[:, j, :], hidden_rows(u)[:, j, :], ident_b[:])

        def copy_x(u):
            made["x_w_rz", u] = stage.tile([P, (B + 2 * H) * PACK], BF16, name="x_w_rz", align_bytes=64)
            interleave(nc.scalar.copy, made["x_w_rz", u][:, 0:B * PACK], made["x_t", u])

        def copy_w_rz(u, copy=nc.scalar.copy):
            copy(out=made["x_w_rz", u][:, B * PACK:(B + 2 * H) * PACK].bitcast(F32).rearrange(
                     "p (c a w) -> p c a w", a=2, w=WORDS),
                 in_=made["w_rz_t", u][:].rearrange("p a w c -> p c a w"))

        def copy_w_n(u):
            made["w_n", u] = stage.tile([P, H * PACK], BF16, name="w_n", align_bytes=64)
            copy = nc.scalar.copy if u == U - 1 else nc.vector.tensor_copy
            copy(out=made["w_n", u][:].bitcast(F32).rearrange("p (c w) -> p c w", w=WORDS),
                 in_=made["w_n_t", u][:, 0:WORDS * P].rearrange("p (w c) -> p c w", w=WORDS))

        def copy_hidden(u):
            made["hidden", u] = keep.tile([P, J, P], BF16, name="hidden%d" % u)
            nc.scalar.copy(out=made["hidden", u][:], in_=made["hidden_t", u][:])

        def copy_w_hh(u):
            made["w_hh", u] = keep.tile([P, GATES * P], BF16, name="w_hh%d" % u)
            copy = nc.scalar.copy if u == U - 1 else nc.vector.tensor_copy
            copy(out=made["w_hh", u][:], in_=w_hh_t(u))

        def hidden_t(u):
            return made["hidden", u][:].rearrange("p j b -> p (j b)")

        def quantise(u, name):
            columns = made[name, u].shape[1] // PACK
            codes = quant.tile([P, columns], U32, name=name + "_codes", align_bytes=64)
            scales = quant.tile([P, columns], U8, name=name + "_scales", align_bytes=64)
            nc.vector.quantize_mx(out=codes[:].bitcast(FP8X4), scales=scales[:], in_=made[name, u][:])
            made[name + "_q", u] = (codes, scales)

        def matmul_x(u, acc, weights, first):
            x_codes, x_scales = made["x_w_rz_q", u]
            w_codes, w_scales = weights
            nc.tensor.matmul_mx(out=acc,
                                lhsT=w_codes[:, first:first + H].bitcast(FP8X4),
                                lhsT_scale=w_scales[:, first:first + H],
                                rhs=x_codes[:, 0:B].bitcast(FP8X4), rhs_scale=x_scales[:, 0:B],
                                start=True, stop=True)

        def matmul_h(u, acc, g):
            nc.tensor.matmul(out=acc, lhsT=made["w_hh", u][:, g * P:(g + 1) * P], rhs=hidden_t(u), start=True, stop=True)

        def matmul_h_rz(u, g):
            ps = bank("h_rz", u, [P, 2 * B], F32, "w_rz_t" if u == U - 1 else "h_rz")
            matmul_h(u, ps[:, g * B:(g + 1) * B], g)

        def matmul_x_rz(u, g):
            ps = bank("x_rz", u, [P, 2 * B], F32, "x_t" if u == U - 1 else "x_rz")
            matmul_x(u, ps[:, g * B:(g + 1) * B], made["x_w_rz_q", u], B + g * H)

        def hx_n_tag(u):
            return {U - 2: "h_rz", U - 1: "w_n_t"}.get(u, "hx_n")

        def matmul_h_n(u):
            matmul_h(u, bank("hx_n", u, [P, 2 * B], F32, hx_n_tag(u))[:, 0:B], 2)

        def matmul_x_n(u):
            ps = bank("hx_n", u, [P, 2 * B], F32, hx_n_tag(u))
            matmul_x(u, ps[:, B:2 * B], made["w_n_q", u], 0)

        def copy_h_rz(u):
            nc.scalar.copy(out=values("h_rz_sb", u, 2 * B)[:], in_=made["h_rz", u][:])

        def add_rz(u, first=0, last=2 * B):
            nc.vector.tensor_tensor(out=values("rz", u, 2 * B)[:, first:last], in0=made["x_rz", u][:, first:last],
                                    in1=made["h_rz_sb", u][:, first:last], op=ALU.add)

        def reset_gate(u, first=0, last=B):
            nc.scalar.activation(out=values("r", u, B)[:, first:last], in_=made["rz", u][:, first:last],
                                 func=ACT.Sigmoid, bias=column(bias_sum, u * GATES), scale=1.0)

        def update_gate(u):
            nc.scalar.activation(out=values("one_minus_z", u, B)[:], in_=made["rz", u][:, B:2 * B],
                                 func=ACT.Sigmoid, bias=column(bias_neg, u * GATES + 1), scale=-1.0)

        def reset_times_hn(u, first=0, last=B):
            nc.vector.scalar_tensor_tensor(out=values("r_hn", u, B)[:, first:last], in0=made["hx_n", u][:, first:last],
                                           scalar=column(bias_cols, (U + u) * GATES + 2),
                                           in1=made["r", u][:, first:last], op0=ALU.add, op1=ALU.mult)

        def add_xn(u, first=0, last=B):
            nc.vector.tensor_tensor(out=values("n_sum", u, B)[:, first:last], in0=made["hx_n", u][:, B + first:B + last],
                                    in1=made["r_hn", u][:, first:last], op=ALU.add)

        def new_gate(u, first=0, last=B):
            nc.scalar.activation(out=values("n", u, B)[:, first:last], in_=made["n_sum", u][:, first:last],
                                 func=ACT.Tanh, bias=column(bias_cols, u * GATES + 2), scale=1.0)

        def subtract_hidden(u, engine, first=0, last=B):
            engine.tensor_tensor(out=values("n_minus_h", u, B)[:, first:last], in0=made["n", u][:, first:last],
                                 in1=hidden_t(u)[:, first:last], op=ALU.subtract)

        def times_update(u, engine, first=0, last=B):
            engine.tensor_tensor(out=values("step", u, B)[:, first:last], in0=made["one_minus_z", u][:, first:last],
                                 in1=made["n_minus_h", u][:, first:last], op=ALU.mult)

        def blend(u, engine):
            subtract_hidden(u, engine)
            times_update(u, engine)

        def transpose_back(u, blocks=range(J)):
            ps = bank("step_t", u, [P, J, H], F32, {U - 3: "hidden_t", U - 2: "hx_n", U - 1: "x_rz"}.get(u, "step_t"))
            for j in blocks:
                nc.tensor.transpose(ps[:, j, :], made["step", u][:, j * P:(j + 1) * P], ident_f[:])

        def add_hidden(u, first=0, last=J):
            if ("out", u // 2) not in made:
                made["out", u // 2] = keep.tile([P, J, 2 * H], F32, name="out%d" % (u // 2))
            nc.vector.tensor_tensor(out=made["out", u // 2][:, first:last, (u % 2) * H:(u % 2 + 1) * H],
                                    in0=made["step_t", u][:, first:last, :], in1=hidden_rows(u)[:, first:last, :],
                                    op=ALU.add)

        def store_pair(u):
            nc.sync.dma_start(out=out_view[:, :, (u - 1) * H:(u + 1) * H], in_=made["out", u // 2][:])

        def store(u, first=0, last=J):
            nc.sync.dma_start(out=out_view[:, first:last, u * H:(u + 1) * H],
                              in_=made["out", u // 2][:, first:last, (u % 2) * H:(u % 2 + 1) * H])

        def add_hidden_and_store(u):
            add_hidden(u)
            if u % 2 == 1:
                store_pair(u)

        def run(step, u, *rest):
            if 0 <= u < U:
                step(u, *rest)

        for i in range(-2, U - 2):
            run(copy_w_n, i + 1)
            run(copy_w_hh, i + 1)
            run(copy_x, i + 1)
            run(copy_w_rz, i + 1)
            run(copy_h_rz, i)
            run(reset_gate, i - 1)
            run(new_gate, i - 2)
            run(copy_hidden, i + 1)
            run(update_gate, i - 2)

            run(matmul_x_n, i - 1)
            run(matmul_h_n, i - 1)
            run(transpose_x, i + 2)
            run(transpose_w_rz, i + 2)
            run(transpose_back, i - 3)

            run(quantise, i + 1, "x_w_rz")
            run(add_rz, i)
            run(reset_times_hn, i - 1)
            run(quantise, i + 1, "w_n")
            run(add_xn, i - 1)
            run(add_hidden_and_store, i - 3)
            run(blend, i - 2, nc.gpsimd)

            run(matmul_h_rz, i + 1, 0)
            run(matmul_h_rz, i + 1, 1)
            run(transpose_w_n, i + 2)
            run(transpose_w_hh, i + 2)
            run(transpose_hidden, i + 2)
            run(matmul_x_rz, i + 1, 0)
            run(matmul_x_rz, i + 1, 1)
            if i == -1:
                bias_ps = transpose_biases()
            elif i == 0:
                prepare_biases(bias_ps)

        z, a, b, c, d = range(U - 5, U)
        halves = [(j * P, (j + 1) * P) for j in range(J)]
        copy_x(d)
        copy_w_rz(d)
        copy_h_rz(c)
        copy_hidden(d)
        copy_w_hh(d)
        reset_gate(b)
        copy_w_n(d)
        new_gate(a)
        matmul_h_n(b)
        matmul_x_n(b)
        transpose_back(z)
        matmul_h_n(c)
        matmul_x_n(c)
        matmul_h_rz(d, 0)
        matmul_h_rz(d, 1)
        quantise(d, "x_w_rz")
        matmul_x_rz(d, 0)
        matmul_x_rz(d, 1)
        add_rz(c)
        reset_gate(c)
        copy_h_rz(d)
        reset_times_hn(b)
        quantise(d, "w_n")
        add_xn(b)
        update_gate(a)
        new_gate(b)
        update_gate(b)
        add_hidden_and_store(z)
        reset_times_hn(c)
        matmul_x_n(d)
        matmul_h_n(d)
        add_rz(d, 0, B)
        blend(a, nc.gpsimd)
        for first, last in halves:
            reset_gate(d, first, last)
        add_xn(c)
        add_rz(d, B, 2 * B)
        new_gate(c)
        update_gate(c)
        update_gate(d)
        transpose_back(a)
        subtract_hidden(b, nc.gpsimd)
        for first, last in halves:
            reset_times_hn(d, first, last)
        for first, last in halves:
            add_xn(d, first, last)
            new_gate(d, first, last)
        subtract_hidden(c, nc.vector)
        times_update(b, nc.vector)
        add_hidden_and_store(a)
        times_update(c, nc.vector)
        transpose_back(b)
        transpose_back(c)
        for first, last in halves:
            subtract_hidden(d, nc.vector, first, last)
        add_hidden_and_store(b)
        for j, (first, last) in enumerate(halves):
            times_update(d, nc.vector, first, last)
            transpose_back(d, (j,))
        add_hidden(c)
        store(c)
        for j in range(J):
            add_hidden(d, j, j + 1)
            store(d, j, j + 1)
